import numpy as np
import ml_dtypes


def mxq(x, axis, fmt="e4m3"):
    dtype, down = {"e4m3": (ml_dtypes.float8_e4m3fn, 7), "e5m2": (ml_dtypes.float8_e5m2, 14)}[fmt]
    v = np.moveaxis(np.asarray(x, np.float32).astype(ml_dtypes.bfloat16).astype(np.float64), axis, -1)
    blocks = v.reshape(v.shape[:-1] + (-1, 32))
    amax = np.abs(blocks).max(-1, keepdims=True)
    byte = np.maximum(np.where(amax > 0, np.frexp(amax)[1] - 1 + 127, 0) - down, 1)
    scale = np.exp2(byte - 127.0)
    codes = (blocks / scale).astype(np.float32).astype(dtype).astype(np.float64)
    return np.moveaxis((codes * scale).reshape(v.shape), -1, axis)


WIDE = False


def mx_kscale(k):
    if not WIDE:
        return np.ones(k)
    levels = np.array([10, -10, 5, -5, 0])
    a = np.random.permutation(np.resize(levels, k // 512 * 4)).reshape(k // 512, 4)
    idx = np.arange(k)
    return np.exp2(a[idx // 512, idx % 128 // 32])


BF16 = ml_dtypes.bfloat16


def bf(x):
    return np.asarray(x, np.float32).astype(BF16)


def f64(x):
    return np.asarray(x).astype(np.float64)


E2M1 = np.array([0.0, 0.5, 1.0, 1.5, 2.0, 3.0, 4.0, 6.0, -0.0, -0.5, -1.0, -1.5, -2.0, -3.0, -4.0, -6.0])


def pack_weight(w, fmt):
    k, n = w.shape
    w = f64(bf(w)).reshape(k // 32, 32, n)
    amax = np.abs(w).max(1)
    if fmt == "e4m3":
        byte = np.frexp(amax)[1] - 1 + 127 - 7
    else:
        mant, ex = np.frexp(amax / 6.0)
        byte = np.where(mant > 0.5, ex, ex - 1) + 127
    byte = np.clip(np.where(amax > 0, byte, 1), 1, 254)
    scaled = (w * np.exp2(127.0 - byte)[:, None, :]).reshape(k, n).astype(np.float32)
    by_word = np.ascontiguousarray(scaled.reshape(k // 512, 128, 4, n).transpose(0, 1, 3, 2))
    if fmt == "e4m3":
        words = by_word.astype(ml_dtypes.float8_e4m3fn).view(np.uint8)
    else:
        c = by_word.astype(ml_dtypes.float4_e2m1fn).view(np.uint8) & 0xF
        words = c[..., 0::2] | (c[..., 1::2] << 4)
    return np.ascontiguousarray(words), np.ascontiguousarray(byte.astype(np.uint8).reshape(k // 512, 16, n))


def unpack_weight(words, scales, fmt):
    g, p, n, _ = words.shape
    if fmt == "e4m3":
        vals = np.ascontiguousarray(words).view(ml_dtypes.float8_e4m3fn).astype(np.float64)
    else:
        nib = np.empty((g, p, n, 4), np.uint8)
        nib[..., 0::2] = words & 0xF
        nib[..., 1::2] = words >> 4
        vals = E2M1[nib]
    vals = vals * np.repeat(np.exp2(scales.astype(np.float64) - 127.0), 8, axis=1)[..., None]
    return vals.transpose(0, 1, 3, 2).reshape(g * 512, n)


B, IN, H = 128, 1024, 2048
MXPASS = 512
QH = H % MXPASS == 0
FMT = "e4m3"


def sigmoid(v):
    return 1.0 / (1.0 + np.exp(-v))


def setup_inputs():
    s = mx_kscale(IN)
    t = mx_kscale(H) if QH else np.ones(H)
    inp = {"x": bf(np.random.standard_normal((B, IN)) * s),
           "h": bf(np.random.standard_normal((B, H)) * t),
           "c": bf(np.random.standard_normal((B, H)))}
    for g in "ifgo":
        wi = np.random.standard_normal((H, IN)) / np.sqrt(IN) / s
        inp["Wi" + g + "_words"], inp["Wi" + g + "_scales"] = pack_weight(np.ascontiguousarray(wi.T), FMT)
        inp["bi" + g] = bf(np.random.standard_normal(H) * 0.3)
        wh = np.random.standard_normal((H, H)) / np.sqrt(H) / t
        inp["Wh" + g + "_words"], inp["Wh" + g + "_scales"] = pack_weight(np.ascontiguousarray(wh.T), FMT)
        inp["bh" + g] = bf(np.random.standard_normal(H) * 0.3)
    return inp


def reference(x, h, c, Wii_words, Wii_scales, bii, Whi_words, Whi_scales, bhi,
              Wif_words, Wif_scales, bif, Whf_words, Whf_scales, bhf,
              Wig_words, Wig_scales, big, Whg_words, Whg_scales, bhg,
              Wio_words, Wio_scales, bio, Who_words, Who_scales, bho):
    Wx = np.concatenate([unpack_weight(Wii_words, Wii_scales, FMT).T, unpack_weight(Wif_words, Wif_scales, FMT).T,
                         unpack_weight(Wig_words, Wig_scales, FMT).T, unpack_weight(Wio_words, Wio_scales, FMT).T], axis=0)
    Wh = np.concatenate([unpack_weight(Whi_words, Whi_scales, FMT).T, unpack_weight(Whf_words, Whf_scales, FMT).T,
                         unpack_weight(Whg_words, Whg_scales, FMT).T, unpack_weight(Who_words, Who_scales, FMT).T], axis=0)
    bx = np.concatenate([f64(bii), f64(bif), f64(big), f64(bio)])
    bh = np.concatenate([f64(bhi), f64(bhf), f64(bhg), f64(bho)])
    px = mxq(f64(x), 1, "e4m3") @ Wx.T
    if QH:
        ph = mxq(f64(h), 1, "e4m3") @ Wh.T
    else:
        ph = f64(h) @ Wh.T
    gates = px + ph + bx + bh
    ii, ff, gg, oo = np.split(gates, 4, axis=-1)
    i = sigmoid(ii)
    f = sigmoid(ff)
    g = np.tanh(gg)
    o = sigmoid(oo)
    c_new = f * f64(c) + i * g
    h_new = o * np.tanh(c_new)
    return np.stack([h_new, c_new])

@@ -1,0 +1,236 @@
+from contextlib import ExitStack
+
+import concourse.mybir as mybir
+from concourse.masks import make_identity
+
+F32 = mybir.dt.float32
+BF16 = mybir.dt.bfloat16
+I32 = mybir.dt.int32
+U32 = mybir.dt.uint32
+U8 = mybir.dt.uint8
+FP8X4 = mybir.dt.float8_e4m3fn_x4
+ACT = mybir.ActivationFunctionType
+ALU = mybir.AluOpType
+
+P = 128
+IN = 1024
+H = 2048
+KP = 512
+NX = IN // KP
+NH = H // KP
+NC = NX + NH
+NT = 512
+NJ = H // NT
+NG = 4
+NB = 12
+NTILES = NG * NC
+FLOPS = 2 * P * (IN + H) * NG * H
+
+
+def tile_lstmcell_w_kernel(
+    tc, x, h, c,
+    Wii_words, Wii_scales, bii, Whi_words, Whi_scales, bhi,
+    Wif_words, Wif_scales, bif, Whf_words, Whf_scales, bhf,
+    Wig_words, Wig_scales, big, Whg_words, Whg_scales, bhg,
+    Wio_words, Wio_scales, bio, Who_words, Who_scales, bho,
+    out,
+):
+    nc = tc.nc
+    wi_words = (Wii_words, Wig_words, Wif_words, Wio_words)
+    wi_scales = (Wii_scales, Wig_scales, Wif_scales, Wio_scales)
+    wh_words = (Whi_words, Whg_words, Whf_words, Who_words)
+    wh_scales = (Whi_scales, Whg_scales, Whf_scales, Who_scales)
+    b_in = (bii, big, bif, bio)
+    b_hid = (bhi, bhg, bhf, bho)
+    funcs = (ACT.Sigmoid, ACT.Tanh, ACT.Sigmoid, ACT.Sigmoid)
+
+    with ExitStack() as ctx:
+        const = ctx.enter_context(tc.tile_pool(name="const", bufs=1))
+        wpool = ctx.enter_context(tc.tile_pool(name="wpool", bufs=NB))
+        lpool = ctx.enter_context(tc.tile_pool(name="lpool", bufs=NJ))
+        aux = ctx.enter_context(tc.psum_pool(name="aux", bufs=2))
+        accp = ctx.enter_context(tc.psum_pool(name="accp", bufs=6))
+        ctx.enter_context(tc.manual_schedule())
+
+        planes = const.tile([P, 6, H], U8, name="planes", align_bytes=64)
+        ones = const.tile([P, P], BF16, name="ones")
+        ident = const.tile([P, P], F32, name="ident")
+        bts = [const.tile([P, H], BF16, name="bt%d" % g) for g in range(NG)]
+        xh = const.tile([P, IN + H], BF16, name="xh")
+        grouped = const.tile([P, NC, P, 4], BF16, name="grouped", align_bytes=64)
+        codes = const.tile([P, NC * P], U32, name="codes", align_bytes=64)
+        xs = const.tile([P, NC * P], U8, name="xs", align_bytes=64)
+        bias_sb = const.tile([P, NG, H], F32, name="bias_sb")
+        c_sb = const.tile([P, H], BF16, name="c_sb")
+        t_i = const.tile([P, H], F32, name="t_i")
+        t_g = const.tile([P, H], F32, name="t_g")
+        t_f = const.tile([P, H], F32, name="t_f")
+        t_c = const.tile([P, H], F32, name="t_c")
+        t_o = const.tile([P, H], F32, name="t_o")
+        gate_tiles = (t_i, t_g, t_f, t_o)
+
+        def cols(j):
+            return slice(NT * j, NT * (j + 1))
+
+        def zero_plane(s):
+            nc.vector.memset(planes[:, s, :].bitcast(I32), 0)
+
+        def zero_bt(g):
+            nc.vector.memset(bts[g][:].bitcast(I32), 0)
+
+        zero_plane(4)
+        zero_plane(0)
+        zero_bt(0)
+        nc.vector.memset(ones[:], 1.0)
+        for s in (1, 5, 2, 3):
+            zero_plane(s)
+        for g in (1, 2, 3):
+            zero_bt(g)
+
+        make_identity(nc, ident[:])
+        pf = planes[:].bitcast(F32)
+        for g in range(NG):
+            si = wi_scales[g].bitcast(F32)
+            sh = wh_scales[g].bitcast(F32)
+            k0 = 8 * (g % 2)
+            for q in range(4):
+                nc.gpsimd.dma_start(
+                    out=pf[32 * q + k0:32 * q + k0 + 4 * NX, 4 + g // 2, :],
+                    in_=si[:, 4 * q:4 * q + 4, :],
+                )
+            for q in range(4):
+                nc.gpsimd.dma_start(
+                    out=pf[32 * q:32 * q + 4 * NH, g, :],
+                    in_=sh[:, 4 * q:4 * q + 4, :],
+                )
+
+        w_tiles = {}
+
+        def load_bias(g):
+            nc.sync.dma_start(out=bts[g][0:1, :], in_=b_in[g].unsqueeze(0))
+            nc.sync.dma_start(out=bts[g][1:2, :], in_=b_hid[g].unsqueeze(0))
+
+        def load_tile(n):
+            g, cc = divmod(n, NC)
+            words = wi_words[g][cc] if cc < NX else wh_words[g][cc - NX]
+            src = words.rearrange("p n t -> p (n t)").bitcast(I32)
+            if n == NTILES - 1:
+                parts = []
+                for j in range(NJ):
+                    wl = lpool.tile([P, NT], U32, name="wl", tag="wl", align_bytes=64)
+                    nc.sync.dma_start(out=wl[:].bitcast(I32), in_=src[:, cols(j)])
+                    parts.append(wl[:])
+                w_tiles[n] = parts
+            else:
+                w = wpool.tile([P, H], U32, name="w", tag="w", align_bytes=64)
+                nc.sync.dma_start(out=w[:].bitcast(I32), in_=src)
+                w_tiles[n] = [w[:, cols(j)] for j in range(NJ)]
+
+        nc.sync.dma_start(out=xh[:, 0:IN], in_=x)
+        nc.sync.dma_start(out=xh[:, IN:IN + H], in_=h)
+        load_bias(0)
+        for n in range(0, 4):
+            load_tile(n)
+        load_bias(1)
+        for n in range(4, 6):
+            load_tile(n)
+        nc.sync.dma_start(out=c_sb[:], in_=c)
+        load_bias(2)
+        for n in range(6, 8):
+            load_tile(n)
+        load_bias(3)
+        for n in range(8, NB):
+            load_tile(n)
+
+        xw = xh[:].bitcast(F32)
+        gw = grouped[:].bitcast(F32)
+
+        def transpose_pair(t):
+            tp = aux.tile([P, 2, 2, P], F32, name="tp", tag="aux")
+            for ci in range(2):
+                cc = 2 * t + ci
+                for u in range(2):
+                    nc.tensor.transpose(
+                        tp[:, ci, u, :], xw[:, 256 * cc + u:256 * (cc + 1):2], ident[:]
+                    )
+            nc.vector.tensor_copy(
+                out=gw[:, 2 * t:2 * t + 2, :, :], in_=tp[:].rearrange("p c u b -> p c b u")
+            )
+
+        def quantise(c0, c1):
+            nc.vector.quantize_mx(
+                out=codes[:, P * c0:P * c1].bitcast(FP8X4),
+                scales=xs[:, P * c0:P * c1],
+                in_=grouped[:, c0:c1, :, :].rearrange("p c b t -> p (c b t)"),
+            )
+
+        transpose_pair(0)
+        transpose_pair(1)
+        quantise(0, NX)
+        transpose_pair(2)
+        quantise(NX, NC)
+
+        def bias_sum(g):
+            for j in range(NJ):
+                bp = aux.tile([P, NT], F32, name="bp", tag="aux")
+                nc.tensor.matmul(out=bp[:], lhsT=ones[:], rhs=bts[g][:, cols(j)], start=True, stop=True)
+                nc.scalar.copy(out=bias_sb[:, g, cols(j)], in_=bp[:])
+
+        acc = {}
+
+        def one_pass(n, j):
+            g, cc = divmod(n, NC)
+            if cc < NX:
+                slot, k = 4 + g // 2, 8 * (g % 2) + 4 * cc
+            else:
+                slot, k = g, 4 * (cc - NX)
+            nc.tensor.matmul_mx(
+                out=acc[g][j][:],
+                lhsT=codes[:, P * cc:P * (cc + 1)].bitcast(FP8X4),
+                lhsT_scale=xs[:, P * cc:P * (cc + 1)],
+                rhs=w_tiles[n][j].bitcast(FP8X4),
+                rhs_scale=planes[k:P, slot, cols(j)],
+                start=(cc == 0),
+                stop=(cc == NC - 1),
+            )
+
+        def pre_act(g, j):
+            dst = gate_tiles[g]
+            nc.vector.tensor_tensor(
+                out=dst[:, cols(j)], in0=acc[g][j][:], in1=bias_sb[:, g, cols(j)], op=ALU.add
+            )
+            nc.scalar.activation(out=dst[:, cols(j)], in_=dst[:, cols(j)], func=funcs[g])
+
+        def post(g, j):
+            cj = cols(j)
+            if g == 1:
+                nc.vector.tensor_tensor(out=t_i[:, cj], in0=t_i[:, cj], in1=t_g[:, cj], op=ALU.mult)
+            elif g == 2:
+                nc.vector.tensor_tensor(out=t_f[:, cj], in0=t_f[:, cj], in1=c_sb[:, cj], op=ALU.mult)
+                nc.vector.tensor_tensor(out=t_f[:, cj], in0=t_f[:, cj], in1=t_i[:, cj], op=ALU.add)
+                nc.scalar.activation(out=t_c[:, cj], in_=t_f[:, cj], func=ACT.Tanh)
+            elif g == 3:
+                nc.vector.tensor_tensor(out=t_o[:, cj], in0=t_o[:, cj], in1=t_c[:, cj], op=ALU.mult)
+                nc.sync.dma_start(out=out[0, :, cj], in_=t_o[:, cj])
+
+        bias_sum(0)
+        for n in range(NTILES):
+            g, cc = divmod(n, NC)
+            if cc == 0:
+                acc[g] = [accp.tile([P, NT], F32, name="acc", tag="acc") for j in range(NJ)]
+            if cc < NC - 1:
+                for j in range(NJ):
+                    one_pass(n, j)
+            else:
+                for j in range(NJ):
+                    one_pass(n, j)
+                    pre_act(g, j)
+                    if j >= 1:
+                        post(g, j - 1)
+                post(g, NJ - 1)
+                if g == 2:
+                    nc.sync.dma_start(out=out[1, :, :], in_=t_f[:])
+            if n in (6, 8, 10):
+                bias_sum(n // 2 - 2)
+            if n + NB < NTILES:
+                load_tile(n + NB)

@@ -89,15 +89,9 @@ def tile_lstmcell_w_kernel(
 
         make_identity(nc, ident[:])
         pf = planes[:].bitcast(F32)
+        pi = planes[:].bitcast(I32)
         for g in range(NG):
-            si = wi_scales[g].bitcast(F32)
             sh = wh_scales[g].bitcast(F32)
-            k0 = 8 * (g % 2)
-            for q in range(4):
-                nc.gpsimd.dma_start(
-                    out=pf[32 * q + k0:32 * q + k0 + 4 * NX, 4 + g // 2, :],
-                    in_=si[:, 4 * q:4 * q + 4, :],
-                )
             for q in range(4):
                 nc.gpsimd.dma_start(
                     out=pf[32 * q:32 * q + 4 * NH, g, :],
@@ -109,6 +103,15 @@ def tile_lstmcell_w_kernel(
         def load_bias(g):
             nc.sync.dma_start(out=bts[g][0:1, :], in_=b_in[g].unsqueeze(0))
             nc.sync.dma_start(out=bts[g][1:2, :], in_=b_hid[g].unsqueeze(0))
+
+        def load_wi_scales(g):
+            si = wi_scales[g].bitcast(I32)
+            k0 = 8 * (g % 2)
+            for q in range(4):
+                nc.sync.dma_start(
+                    out=pi[32 * q + k0:32 * q + k0 + 4 * NX, 4 + g // 2, :],
+                    in_=si[:, 4 * q:4 * q + 4, :],
+                )
 
         def load_tile(n):
             g, cc = divmod(n, NC)
@@ -128,18 +131,24 @@ def tile_lstmcell_w_kernel(
 
         nc.sync.dma_start(out=xh[:, 0:IN], in_=x)
         nc.sync.dma_start(out=xh[:, IN:IN + H], in_=h)
+        load_tile(0)
+        load_wi_scales(0)
+        load_tile(1)
         load_bias(0)
-        for n in range(0, 4):
-            load_tile(n)
+        load_tile(2)
+        load_tile(3)
         load_bias(1)
-        for n in range(4, 6):
-            load_tile(n)
+        load_tile(4)
+        load_wi_scales(1)
+        load_tile(5)
         nc.sync.dma_start(out=c_sb[:], in_=c)
         load_bias(2)
-        for n in range(6, 8):
-            load_tile(n)
+        load_tile(6)
+        load_tile(7)
         load_bias(3)
-        for n in range(8, NB):
+        load_tile(8)
+        load_wi_scales(2)
+        for n in range(9, NB):
             load_tile(n)
 
         xw = xh[:].bitcast(F32)
@@ -234,3 +243,5 @@ def tile_lstmcell_w_kernel(
                 bias_sum(n // 2 - 2)
             if n + NB < NTILES:
                 load_tile(n + NB)
+            if n == 1:
+                load_wi_scales(3)

@@ -78,25 +78,15 @@ def tile_lstmcell_w_kernel(
         def zero_bt(g):
             nc.vector.memset(bts[g][:].bitcast(I32), 0)
 
-        zero_plane(4)
-        zero_plane(0)
+        for s in (4, 0, 1, 5, 2, 3):
+            zero_plane(s)
         zero_bt(0)
         nc.vector.memset(ones[:], 1.0)
-        for s in (1, 5, 2, 3):
-            zero_plane(s)
         for g in (1, 2, 3):
             zero_bt(g)
 
         make_identity(nc, ident[:])
-        pf = planes[:].bitcast(F32)
         pi = planes[:].bitcast(I32)
-        for g in range(NG):
-            sh = wh_scales[g].bitcast(F32)
-            for q in range(4):
-                nc.gpsimd.dma_start(
-                    out=pf[32 * q:32 * q + 4 * NH, g, :],
-                    in_=sh[:, 4 * q:4 * q + 4, :],
-                )
 
         w_tiles = {}
 
@@ -104,13 +94,19 @@ def tile_lstmcell_w_kernel(
             nc.sync.dma_start(out=bts[g][0:1, :], in_=b_in[g].unsqueeze(0))
             nc.sync.dma_start(out=bts[g][1:2, :], in_=b_hid[g].unsqueeze(0))
 
-        def load_wi_scales(g):
+        def load_scales(g):
             si = wi_scales[g].bitcast(I32)
             k0 = 8 * (g % 2)
-            for q in range(4):
+            for q in (0, 2, 1, 3):
                 nc.sync.dma_start(
                     out=pi[32 * q + k0:32 * q + k0 + 4 * NX, 4 + g // 2, :],
                     in_=si[:, 4 * q:4 * q + 4, :],
+                )
+            sh = wh_scales[g].bitcast(I32)
+            for q in (0, 2, 1, 3):
+                nc.sync.dma_start(
+                    out=pi[32 * q:32 * q + 4 * NH, g, :],
+                    in_=sh[:, 4 * q:4 * q + 4, :],
                 )
 
         def load_tile(n):
@@ -131,24 +127,22 @@ def tile_lstmcell_w_kernel(
 
         nc.sync.dma_start(out=xh[:, 0:IN], in_=x)
         nc.sync.dma_start(out=xh[:, IN:IN + H], in_=h)
-        load_tile(0)
-        load_wi_scales(0)
-        load_tile(1)
+        for g in range(NG):
+            load_scales(g)
         load_bias(0)
+        load_tile(0)
+        load_tile(1)
         load_tile(2)
         load_tile(3)
         load_bias(1)
         load_tile(4)
-        load_wi_scales(1)
         load_tile(5)
         nc.sync.dma_start(out=c_sb[:], in_=c)
         load_bias(2)
         load_tile(6)
         load_tile(7)
         load_bias(3)
-        load_tile(8)
-        load_wi_scales(2)
-        for n in range(9, NB):
+        for n in range(8, NB):
             load_tile(n)
 
         xw = xh[:].bitcast(F32)
@@ -243,5 +237,3 @@ def tile_lstmcell_w_kernel(
                 bias_sum(n // 2 - 2)
             if n + NB < NTILES:
                 load_tile(n + NB)
-            if n == 1:
-                load_wi_scales(3)

@@ -78,15 +78,22 @@ def tile_lstmcell_w_kernel(
         def zero_bt(g):
             nc.vector.memset(bts[g][:].bitcast(I32), 0)
 
-        for s in (4, 0, 1, 5, 2, 3):
+        for s in (0, 4, 1, 2, 3, 5):
             zero_plane(s)
         zero_bt(0)
         nc.vector.memset(ones[:], 1.0)
-        for g in (1, 2, 3):
-            zero_bt(g)
 
         make_identity(nc, ident[:])
         pi = planes[:].bitcast(I32)
+        pf = planes[:].bitcast(F32)
+        for g in range(NG):
+            si = wi_scales[g].bitcast(F32)
+            k0 = 8 * (g % 2)
+            for q in (0, 2, 1, 3):
+                nc.gpsimd.dma_start(
+                    out=pf[32 * q + k0:32 * q + k0 + 4 * NX, 4 + g // 2, :],
+                    in_=si[:, 4 * q:4 * q + 4, :],
+                )
 
         w_tiles = {}
 
@@ -95,13 +102,6 @@ def tile_lstmcell_w_kernel(
             nc.sync.dma_start(out=bts[g][1:2, :], in_=b_hid[g].unsqueeze(0))
 
         def load_scales(g):
-            si = wi_scales[g].bitcast(I32)
-            k0 = 8 * (g % 2)
-            for q in (0, 2, 1, 3):
-                nc.sync.dma_start(
-                    out=pi[32 * q + k0:32 * q + k0 + 4 * NX, 4 + g // 2, :],
-                    in_=si[:, 4 * q:4 * q + 4, :],
-                )
             sh = wh_scales[g].bitcast(I32)
             for q in (0, 2, 1, 3):
                 nc.sync.dma_start(
@@ -134,16 +134,6 @@ def tile_lstmcell_w_kernel(
         load_tile(1)
         load_tile(2)
         load_tile(3)
-        load_bias(1)
-        load_tile(4)
-        load_tile(5)
-        nc.sync.dma_start(out=c_sb[:], in_=c)
-        load_bias(2)
-        load_tile(6)
-        load_tile(7)
-        load_bias(3)
-        for n in range(8, NB):
-            load_tile(n)
 
         xw = xh[:].bitcast(F32)
         gw = grouped[:].bitcast(F32)
@@ -172,6 +162,18 @@ def tile_lstmcell_w_kernel(
         quantise(0, NX)
         transpose_pair(2)
         quantise(NX, NC)
+        for g in (1, 2, 3):
+            zero_bt(g)
+        load_bias(1)
+        load_tile(4)
+        load_tile(5)
+        nc.sync.dma_start(out=c_sb[:], in_=c)
+        load_bias(2)
+        load_tile(6)
+        load_tile(7)
+        load_bias(3)
+        for n in range(8, NB):
+            load_tile(n)
 
         def bias_sum(g):
             for j in range(NJ):

@@ -215,7 +215,8 @@ def tile_lstmcell_w_kernel(
                 nc.vector.tensor_tensor(out=t_f[:, cj], in0=t_f[:, cj], in1=t_i[:, cj], op=ALU.add)
                 nc.scalar.activation(out=t_c[:, cj], in_=t_f[:, cj], func=ACT.Tanh)
             elif g == 3:
-                nc.vector.tensor_tensor(out=t_o[:, cj], in0=t_o[:, cj], in1=t_c[:, cj], op=ALU.mult)
+                eng = nc.gpsimd if j % 2 == 0 else nc.vector
+                eng.tensor_tensor(out=t_o[:, cj], in0=t_o[:, cj], in1=t_c[:, cj], op=ALU.mult)
                 nc.sync.dma_start(out=out[0, :, cj], in_=t_o[:, cj])
 
         bias_sum(0)
@@ -227,12 +228,14 @@ def tile_lstmcell_w_kernel(
                 for j in range(NJ):
                     one_pass(n, j)
             else:
+                lag = NJ if g == 3 else 1
                 for j in range(NJ):
                     one_pass(n, j)
                     pre_act(g, j)
-                    if j >= 1:
-                        post(g, j - 1)
-                post(g, NJ - 1)
+                    if j >= lag:
+                        post(g, j - lag)
+                for j in range(NJ - lag, NJ):
+                    post(g, j)
                 if g == 2:
                     nc.sync.dma_start(out=out[1, :, :], in_=t_f[:])
             if n in (6, 8, 10):

@@ -24,6 +24,7 @@ NJ = H // NT
 NG = 4
 NB = 12
 NTILES = NG * NC
+NSPLIT = 2
 FLOPS = 2 * P * (IN + H) * NG * H
 
 
@@ -47,7 +48,7 @@ def tile_lstmcell_w_kernel(
     with ExitStack() as ctx:
         const = ctx.enter_context(tc.tile_pool(name="const", bufs=1))
         wpool = ctx.enter_context(tc.tile_pool(name="wpool", bufs=NB))
-        lpool = ctx.enter_context(tc.tile_pool(name="lpool", bufs=NJ))
+        lpool = ctx.enter_context(tc.tile_pool(name="lpool", bufs=NSPLIT * NJ))
         aux = ctx.enter_context(tc.psum_pool(name="aux", bufs=2))
         accp = ctx.enter_context(tc.psum_pool(name="accp", bufs=6))
         ctx.enter_context(tc.manual_schedule())
@@ -113,17 +114,22 @@ def tile_lstmcell_w_kernel(
             g, cc = divmod(n, NC)
             words = wi_words[g][cc] if cc < NX else wh_words[g][cc - NX]
             src = words.rearrange("p n t -> p (n t)").bitcast(I32)
-            if n == NTILES - 1:
-                parts = []
-                for j in range(NJ):
-                    wl = lpool.tile([P, NT], U32, name="wl", tag="wl", align_bytes=64)
-                    nc.sync.dma_start(out=wl[:].bitcast(I32), in_=src[:, cols(j)])
-                    parts.append(wl[:])
-                w_tiles[n] = parts
+            if n >= NTILES - NSPLIT:
+                w_tiles[n] = src
             else:
                 w = wpool.tile([P, H], U32, name="w", tag="w", align_bytes=64)
                 nc.sync.dma_start(out=w[:].bitcast(I32), in_=src)
                 w_tiles[n] = [w[:, cols(j)] for j in range(NJ)]
+
+        def load_pieces():
+            srcs = [w_tiles[n] for n in range(NTILES - NSPLIT, NTILES)]
+            for n in range(NTILES - NSPLIT, NTILES):
+                w_tiles[n] = []
+            for j in range(NJ):
+                for i in range(NSPLIT):
+                    wl = lpool.tile([P, NT], U32, name="wl", tag="wl", align_bytes=64)
+                    nc.sync.dma_start(out=wl[:].bitcast(I32), in_=srcs[i][:, cols(j)])
+                    w_tiles[NTILES - NSPLIT + i].append(wl[:])
 
         nc.sync.dma_start(out=xh[:, 0:IN], in_=x)
         nc.sync.dma_start(out=xh[:, IN:IN + H], in_=h)
@@ -215,8 +221,7 @@ def tile_lstmcell_w_kernel(
                 nc.vector.tensor_tensor(out=t_f[:, cj], in0=t_f[:, cj], in1=t_i[:, cj], op=ALU.add)
                 nc.scalar.activation(out=t_c[:, cj], in_=t_f[:, cj], func=ACT.Tanh)
             elif g == 3:
-                eng = nc.gpsimd if j % 2 == 0 else nc.vector
-                eng.tensor_tensor(out=t_o[:, cj], in0=t_o[:, cj], in1=t_c[:, cj], op=ALU.mult)
+                nc.vector.tensor_tensor(out=t_o[:, cj], in0=t_o[:, cj], in1=t_c[:, cj], op=ALU.mult)
                 nc.sync.dma_start(out=out[0, :, cj], in_=t_o[:, cj])
 
         bias_sum(0)
@@ -224,21 +229,30 @@ def tile_lstmcell_w_kernel(
             g, cc = divmod(n, NC)
             if cc == 0:
                 acc[g] = [accp.tile([P, NT], F32, name="acc", tag="acc") for j in range(NJ)]
-            if cc < NC - 1:
+            if n >= NTILES - NSPLIT:
+                if n == NTILES - 1:
+                    for j in range(NJ):
+                        for m in range(NTILES - NSPLIT, NTILES):
+                            one_pass(m, j)
+                        pre_act(g, j)
+                        if j >= 1:
+                            post(g, j - 1)
+                    post(g, NJ - 1)
+            elif cc < NC - 1:
                 for j in range(NJ):
                     one_pass(n, j)
             else:
-                lag = NJ if g == 3 else 1
                 for j in range(NJ):
                     one_pass(n, j)
                     pre_act(g, j)
-                    if j >= lag:
-                        post(g, j - lag)
-                for j in range(NJ - lag, NJ):
-                    post(g, j)
+                    if j >= 1:
+                        post(g, j - 1)
+                post(g, NJ - 1)
                 if g == 2:
                     nc.sync.dma_start(out=out[1, :, :], in_=t_f[:])
             if n in (6, 8, 10):
                 bias_sum(n // 2 - 2)
             if n + NB < NTILES:
                 load_tile(n + NB)
+                if n + NB == NTILES - 1:
+                    load_pieces()

from contextlib import ExitStack

import concourse.mybir as mybir
from concourse.masks import make_identity

F32 = mybir.dt.float32
BF16 = mybir.dt.bfloat16
I32 = mybir.dt.int32
U32 = mybir.dt.uint32
U8 = mybir.dt.uint8
FP8X4 = mybir.dt.float8_e4m3fn_x4
ACT = mybir.ActivationFunctionType
ALU = mybir.AluOpType

P = 128
IN = 1024
H = 2048
KP = 512
NX = IN // KP
NH = H // KP
NC = NX + NH
NT = 512
NJ = H // NT
NG = 4
NB = 12
NTILES = NG * NC
NSPLIT = 2
FLOPS = 2 * P * (IN + H) * NG * H


def tile_lstmcell_w_kernel(
    tc, x, h, c,
    Wii_words, Wii_scales, bii, Whi_words, Whi_scales, bhi,
    Wif_words, Wif_scales, bif, Whf_words, Whf_scales, bhf,
    Wig_words, Wig_scales, big, Whg_words, Whg_scales, bhg,
    Wio_words, Wio_scales, bio, Who_words, Who_scales, bho,
    out,
):
    nc = tc.nc
    wi_words = (Wii_words, Wig_words, Wif_words, Wio_words)
    wi_scales = (Wii_scales, Wig_scales, Wif_scales, Wio_scales)
    wh_words = (Whi_words, Whg_words, Whf_words, Who_words)
    wh_scales = (Whi_scales, Whg_scales, Whf_scales, Who_scales)
    b_in = (bii, big, bif, bio)
    b_hid = (bhi, bhg, bhf, bho)
    funcs = (ACT.Sigmoid, ACT.Tanh, ACT.Sigmoid, ACT.Sigmoid)

    with ExitStack() as ctx:
        const = ctx.enter_context(tc.tile_pool(name="const", bufs=1))
        wpool = ctx.enter_context(tc.tile_pool(name="wpool", bufs=NB))
        lpool = ctx.enter_context(tc.tile_pool(name="lpool", bufs=NSPLIT * NJ))
        aux = ctx.enter_context(tc.psum_pool(name="aux", bufs=2))
        accp = ctx.enter_context(tc.psum_pool(name="accp", bufs=6))
        ctx.enter_context(tc.manual_schedule())

        planes = const.tile([P, 6, H], U8, name="planes", align_bytes=64)
        ones = const.tile([P, P], BF16, name="ones")
        ident = const.tile([P, P], F32, name="ident")
        bts = [const.tile([P, H], BF16, name="bt%d" % g) for g in range(NG)]
        xh = const.tile([P, IN + H], BF16, name="xh")
        grouped = const.tile([P, NC, P, 4], BF16, name="grouped", align_bytes=64)
        codes = const.tile([P, NC * P], U32, name="codes", align_bytes=64)
        xs = const.tile([P, NC * P], U8, name="xs", align_bytes=64)
        bias_sb = const.tile([P, NG, H], F32, name="bias_sb")
        c_sb = const.tile([P, H], BF16, name="c_sb")
        t_i = const.tile([P, H], F32, name="t_i")
        t_g = const.tile([P, H], F32, name="t_g")
        t_f = const.tile([P, H], F32, name="t_f")
        t_c = const.tile([P, H], F32, name="t_c")
        t_o = const.tile([P, H], F32, name="t_o")
        gate_tiles = (t_i, t_g, t_f, t_o)

        def cols(j):
            return slice(NT * j, NT * (j + 1))

        def zero_plane(s):
            nc.vector.memset(planes[:, s, :].bitcast(I32), 0)

        def zero_bt(g):
            nc.vector.memset(bts[g][:].bitcast(I32), 0)

        for s in (0, 4, 1, 2, 3, 5):
            zero_plane(s)
        zero_bt(0)
        nc.vector.memset(ones[:], 1.0)

        make_identity(nc, ident[:])
        pi = planes[:].bitcast(I32)
        pf = planes[:].bitcast(F32)
        for g in range(NG):
            si = wi_scales[g].bitcast(F32)
            k0 = 8 * (g % 2)
            for q in (0, 2, 1, 3):
                nc.gpsimd.dma_start(
                    out=pf[32 * q + k0:32 * q + k0 + 4 * NX, 4 + g // 2, :],
                    in_=si[:, 4 * q:4 * q + 4, :],
                )

        w_tiles = {}

        def load_bias(g):
            nc.sync.dma_start(out=bts[g][0:1, :], in_=b_in[g].unsqueeze(0))
            nc.sync.dma_start(out=bts[g][1:2, :], in_=b_hid[g].unsqueeze(0))

        def load_scales(g):
            sh = wh_scales[g].bitcast(I32)
            for q in (0, 2, 1, 3):
                nc.sync.dma_start(
                    out=pi[32 * q:32 * q + 4 * NH, g, :],
                    in_=sh[:, 4 * q:4 * q + 4, :],
                )

        def load_tile(n):
            g, cc = divmod(n, NC)
            words = wi_words[g][cc] if cc < NX else wh_words[g][cc - NX]
            src = words.rearrange("p n t -> p (n t)").bitcast(I32)
            if n >= NTILES - NSPLIT:
                w_tiles[n] = src
            else:
                w = wpool.tile([P, H], U32, name="w", tag="w", align_bytes=64)
                nc.sync.dma_start(out=w[:].bitcast(I32), in_=src)
                w_tiles[n] = [w[:, cols(j)] for j in range(NJ)]

        def load_pieces():
            srcs = [w_tiles[n] for n in range(NTILES - NSPLIT, NTILES)]
            for n in range(NTILES - NSPLIT, NTILES):
                w_tiles[n] = []
            for j in range(NJ):
                for i in range(NSPLIT):
                    wl = lpool.tile([P, NT], U32, name="wl", tag="wl", align_bytes=64)
                    nc.sync.dma_start(out=wl[:].bitcast(I32), in_=srcs[i][:, cols(j)])
                    w_tiles[NTILES - NSPLIT + i].append(wl[:])

        nc.sync.dma_start(out=xh[:, 0:IN], in_=x)
        nc.sync.dma_start(out=xh[:, IN:IN + H], in_=h)
        for g in range(NG):
            load_scales(g)
        load_bias(0)
        load_tile(0)
        load_tile(1)
        load_tile(2)
        load_tile(3)

        xw = xh[:].bitcast(F32)
        gw = grouped[:].bitcast(F32)

        def transpose_pair(t):
            tp = aux.tile([P, 2, 2, P], F32, name="tp", tag="aux")
            for ci in range(2):
                cc = 2 * t + ci
                for u in range(2):
                    nc.tensor.transpose(
                        tp[:, ci, u, :], xw[:, 256 * cc + u:256 * (cc + 1):2], ident[:]
                    )
            nc.vector.tensor_copy(
                out=gw[:, 2 * t:2 * t + 2, :, :], in_=tp[:].rearrange("p c u b -> p c b u")
            )

        def quantise(c0, c1):
            nc.vector.quantize_mx(
                out=codes[:, P * c0:P * c1].bitcast(FP8X4),
                scales=xs[:, P * c0:P * c1],
                in_=grouped[:, c0:c1, :, :].rearrange("p c b t -> p (c b t)"),
            )

        transpose_pair(0)
        transpose_pair(1)
        quantise(0, NX)
        transpose_pair(2)
        quantise(NX, NC)
        for g in (1, 2, 3):
            zero_bt(g)
        load_bias(1)
        load_tile(4)
        load_tile(5)
        nc.sync.dma_start(out=c_sb[:], in_=c)
        load_bias(2)
        load_tile(6)
        load_tile(7)
        load_bias(3)
        for n in range(8, NB):
            load_tile(n)

        def bias_sum(g):
            for j in range(NJ):
                bp = aux.tile([P, NT], F32, name="bp", tag="aux")
                nc.tensor.matmul(out=bp[:], lhsT=ones[:], rhs=bts[g][:, cols(j)], start=True, stop=True)
                nc.scalar.copy(out=bias_sb[:, g, cols(j)], in_=bp[:])

        acc = {}

        def one_pass(n, j):
            g, cc = divmod(n, NC)
            if cc < NX:
                slot, k = 4 + g // 2, 8 * (g % 2) + 4 * cc
            else:
                slot, k = g, 4 * (cc - NX)
            nc.tensor.matmul_mx(
                out=acc[g][j][:],
                lhsT=codes[:, P * cc:P * (cc + 1)].bitcast(FP8X4),
                lhsT_scale=xs[:, P * cc:P * (cc + 1)],
                rhs=w_tiles[n][j].bitcast(FP8X4),
                rhs_scale=planes[k:P, slot, cols(j)],
                start=(cc == 0),
                stop=(cc == NC - 1),
            )

        def pre_act(g, j):
            dst = gate_tiles[g]
            nc.vector.tensor_tensor(
                out=dst[:, cols(j)], in0=acc[g][j][:], in1=bias_sb[:, g, cols(j)], op=ALU.add
            )
            nc.scalar.activation(out=dst[:, cols(j)], in_=dst[:, cols(j)], func=funcs[g])

        def post(g, j):
            cj = cols(j)
            if g == 1:
                nc.vector.tensor_tensor(out=t_i[:, cj], in0=t_i[:, cj], in1=t_g[:, cj], op=ALU.mult)
            elif g == 2:
                nc.vector.tensor_tensor(out=t_f[:, cj], in0=t_f[:, cj], in1=c_sb[:, cj], op=ALU.mult)
                nc.vector.tensor_tensor(out=t_f[:, cj], in0=t_f[:, cj], in1=t_i[:, cj], op=ALU.add)
                nc.scalar.activation(out=t_c[:, cj], in_=t_f[:, cj], func=ACT.Tanh)
            elif g == 3:
                nc.vector.tensor_tensor(out=t_o[:, cj], in0=t_o[:, cj], in1=t_c[:, cj], op=ALU.mult)
                nc.sync.dma_start(out=out[0, :, cj], in_=t_o[:, cj])

        bias_sum(0)
        for n in range(NTILES):
            g, cc = divmod(n, NC)
            if cc == 0:
                acc[g] = [accp.tile([P, NT], F32, name="acc", tag="acc") for j in range(NJ)]
            if n >= NTILES - NSPLIT:
                if n == NTILES - 1:
                    for j in range(NJ):
                        for m in range(NTILES - NSPLIT, NTILES):
                            one_pass(m, j)
                        pre_act(g, j)
                        if j >= 1:
                            post(g, j - 1)
                    post(g, NJ - 1)
            elif cc < NC - 1:
                for j in range(NJ):
                    one_pass(n, j)
            else:
                for j in range(NJ):
                    one_pass(n, j)
                    pre_act(g, j)
                    if j >= 1:
                        post(g, j - 1)
                post(g, NJ - 1)
                if g == 2:
                    nc.sync.dma_start(out=out[1, :, :], in_=t_f[:])
            if n in (6, 8, 10):
                bias_sum(n // 2 - 2)
            if n + NB < NTILES:
                load_tile(n + NB)
                if n + NB == NTILES - 1:
                    load_pieces()
